import numpy as np
import ml_dtypes


def mxq(x, axis, fmt="e4m3"):
    dtype, down = {"e4m3": (ml_dtypes.float8_e4m3fn, 7), "e5m2": (ml_dtypes.float8_e5m2, 14)}[fmt]
    v = np.moveaxis(np.asarray(x, np.float32).astype(ml_dtypes.bfloat16).astype(np.float64), axis, -1)
    blocks = v.reshape(v.shape[:-1] + (-1, 32))
    amax = np.abs(blocks).max(-1, keepdims=True)
    byte = np.maximum(np.where(amax > 0, np.frexp(amax)[1] - 1 + 127, 0) - down, 1)
    scale = np.exp2(byte - 127.0)
    codes = (blocks / scale).astype(np.float32).astype(dtype).astype(np.float64)
    return np.moveaxis((codes * scale).reshape(v.shape), -1, axis)


WIDE = False


def mx_kscale(k):
    if not WIDE:
        return np.ones(k)
    levels = np.array([10, -10, 5, -5, 0])
    if k % 512:
        return np.exp2(np.random.permutation(np.resize(levels, k // 32))).repeat(32)
    a = np.empty((k // 512, 16))
    for p in range(k // 512):
        a[p, :8] = np.random.permutation(np.resize(levels, 8))
        for g in range(8):
            far = levels[np.abs(levels - a[p, g]) >= 10]
            a[p, g + 8] = far[np.random.randint(len(far))]
    return np.exp2(a.ravel()).repeat(32)


BF16 = ml_dtypes.bfloat16


def bf(x):
    return np.asarray(x, np.float32).astype(BF16)


def f64(x):
    return np.asarray(x).astype(np.float64)


B, R, C, H, DH = 16, 8, 1536, 12, 128
T = R * R
E = H * DH
EPS = 2.0 ** -23


def rmsnorm(v):
    return v * (1.0 / np.sqrt(np.mean(np.square(v), axis=-1, keepdims=True) + EPS))


def setup_inputs():
    s = mx_kscale(C)
    return {"x": bf(np.random.standard_normal((B, T, C)) * s),
            "Wq": bf(np.random.standard_normal((C, E)) / np.sqrt(C) / s[:, None]),
            "Wk": bf(np.random.standard_normal((C, E)) / np.sqrt(C) / s[:, None])}


def reference(x, Wq, Wk):
    xq = mxq(f64(x), 2, "e4m3")

    def proj(W):
        return (xq @ mxq(f64(W), 0, "e4m3")).reshape(B, T, H, DH).transpose(0, 2, 1, 3)

    return rmsnorm(proj(Wq)), rmsnorm(proj(Wk))

@@ -1,0 +1,210 @@
+from contextlib import ExitStack
+
+import concourse.mybir as mybir
+from concourse.masks import make_identity
+
+F32 = mybir.dt.float32
+BF16 = mybir.dt.bfloat16
+U32 = mybir.dt.uint32
+U8 = mybir.dt.uint8
+FP8X4 = mybir.dt.float8_e4m3fn_x4
+ACT = mybir.ActivationFunctionType
+ALU = mybir.AluOpType
+
+P = 128
+PACK = 4
+K_PASS = P * PACK
+BOARDS, SQUARES, C, HEADS, DH = 16, 64, 1536, 12, 128
+TOKENS = BOARDS * SQUARES
+TOKEN_TILES = TOKENS // P
+PASSES = C // K_PASS
+BLOCK = 512
+BLOCK_HEADS = BLOCK // DH
+BLOCKS_PER_WEIGHT = HEADS * DH // BLOCK
+EPS = 2.0 ** -23
+SCALAR_SCALES_EVERY = 3
+STORE_TILES = 4
+SCALE_LAG = 2
+
+FLOPS = 2 * TOKENS * C * 2 * HEADS * DH
+
+
+def tile_pieceroutedattention_pa_kernel(tc, x, Wq, Wk, out_0, out_1):
+    nc = tc.nc
+    blocks = [(w, out, b) for (w, out) in ((Wq, out_0), (Wk, out_1)) for b in range(BLOCKS_PER_WEIGHT)]
+
+    with ExitStack() as ctx:
+        const = ctx.enter_context(tc.tile_pool(name="const", bufs=1))
+        x_raw_pool = ctx.enter_context(tc.tile_pool(name="x_raw", bufs=TOKEN_TILES))
+        x_stage = ctx.enter_context(tc.tile_pool(name="x_stage", bufs=4))
+        w_raw_pool = ctx.enter_context(tc.tile_pool(name="w_raw", bufs=len(blocks) * PASSES))
+        w_stage = ctx.enter_context(tc.tile_pool(name="w_stage", bufs=PASSES))
+        w_mx = ctx.enter_context(tc.tile_pool(name="w_mx", bufs=2))
+        norm = ctx.enter_context(tc.tile_pool(name="norm", bufs=8))
+        squares = ctx.enter_context(tc.tile_pool(name="squares", bufs=4))
+        results = ctx.enter_context(tc.tile_pool(name="results", bufs=3))
+        psum = ctx.enter_context(tc.psum_pool(name="psum", bufs=8))
+
+        ident = const.tile([P, P], F32)
+        make_identity(nc, ident[:])
+
+        def load_block(w, b):
+            pieces = []
+            for g in range(PASSES):
+                w_raw = w_raw_pool.tile([P, PACK, BLOCK], BF16)
+                k0 = K_PASS * g
+                nc.sync.dma_start(
+                    out=w_raw[:],
+                    in_=w[k0 : k0 + K_PASS, BLOCK * b : BLOCK * (b + 1)].rearrange("(q t) c -> q t c", t=PACK),
+                )
+                pieces.append(w_raw)
+            return pieces
+
+        w_raws = [load_block(blocks[0][0], blocks[0][2])]
+        x_by_tile = x.rearrange("b (q j) c -> (b q) j c", j=TOKEN_TILES)
+        x_raws = []
+        for j in range(TOKEN_TILES):
+            x_raw = x_raw_pool.tile([P, C], BF16)
+            nc.sync.dma_start(out=x_raw[:], in_=x_by_tile[:, j, :])
+            x_raws.append(x_raw)
+        for w, out, b in blocks[1:]:
+            w_raws.append(load_block(w, b))
+
+        def new_block_tiles():
+            w_codes = w_mx.tile([P, PASSES, BLOCK], U32, align_bytes=64)
+            w_scales = w_mx.tile([P, PASSES, BLOCK], U8, align_bytes=64)
+            return {"codes": w_codes, "scales": w_scales, "grouped": []}
+
+        def regroup(mx, pieces, g):
+            w_grouped = w_stage.tile([P, BLOCK, PACK], BF16, align_bytes=64)
+            nc.vector.tensor_copy(
+                out=w_grouped[:].rearrange("p (c i) t -> p c t i", i=4),
+                in_=pieces[g][:].rearrange("p t (c i) -> p c t i", i=4),
+            )
+            mx["grouped"].append(w_grouped)
+
+        def quantise(mx, g):
+            nc.vector.quantize_mx(
+                out=mx["codes"][:, g, :].bitcast(FP8X4),
+                scales=mx["scales"][:, g, :],
+                in_=mx["grouped"][g][:].rearrange("p c t -> p (c t)"),
+            )
+
+        def prepare(mx, pieces, turn):
+            if turn < 2 * PASSES:
+                if turn % 2 == 0:
+                    regroup(mx, pieces, turn // 2)
+                else:
+                    quantise(mx, turn // 2)
+
+        w_next = new_block_tiles()
+        for turn in range(2 * PASSES):
+            prepare(w_next, w_raws[0], turn)
+
+        x_codes = const.tile([P, PASSES, TOKENS], U32, align_bytes=64)
+        x_scales = const.tile([P, PASSES, TOKENS], U8, align_bytes=64)
+        for j0 in range(0, TOKEN_TILES, 2):
+            for g in range(PASSES):
+                planes = psum.tile([P, 2, 2, P], F32, tag="bank")
+                for s in range(2):
+                    words = x_raws[j0 + s][:].bitcast(F32)
+                    for u in range(2):
+                        w0 = 2 * P * g
+                        nc.tensor.transpose(planes[:, s, u, :], words[:, w0 + u : w0 + 2 * P : 2], ident[:])
+                x_grouped = x_stage.tile([P, 2 * P * PACK], BF16, align_bytes=64)
+                nc.scalar.copy(
+                    out=x_grouped[:].bitcast(F32).rearrange("p (s r u) -> p s r u", s=2, u=2),
+                    in_=planes[:].rearrange("p s u r -> p s r u"),
+                )
+                tokens = slice(P * j0, P * (j0 + 2))
+                nc.vector.quantize_mx(
+                    out=x_codes[:, g, tokens].bitcast(FP8X4),
+                    scales=x_scales[:, g, tokens],
+                    in_=x_grouped[:],
+                )
+
+        banks = {}
+
+        def products(step, mx, result):
+            j = step % TOKEN_TILES
+            tokens = slice(P * j, P * (j + 1))
+            acc = psum.tile([P, BLOCK], F32, tag="bank")
+            for g in range(PASSES):
+                nc.tensor.matmul_mx(
+                    out=acc[:],
+                    lhsT=x_codes[:, g, tokens].bitcast(FP8X4),
+                    lhsT_scale=x_scales[:, g, tokens],
+                    rhs=mx["codes"][:, g, :].bitcast(FP8X4),
+                    rhs_scale=mx["scales"][:, g, :],
+                    start=(g == 0),
+                    stop=(g == PASSES - 1),
+                )
+            banks[step] = {"acc": acc, "result": result}
+
+        def sums_of_squares(step):
+            acc = banks[step]["acc"]
+            squared = squares.tile([P, BLOCK], BF16)
+            sum_sq = norm.tile([P, BLOCK_HEADS], F32)
+            for h in range(BLOCK_HEADS):
+                cols = slice(DH * h, DH * (h + 1))
+                nc.scalar.activation(
+                    out=squared[:, cols], in_=acc[:, cols], func=ACT.Square, accum_out=sum_sq[:, h : h + 1]
+                )
+            banks[step]["sum_sq"] = sum_sq
+
+        def inverse_rms(step):
+            inv_rms = norm.tile([P, BLOCK_HEADS], F32)
+            nc.scalar.activation(
+                out=inv_rms[:], in_=banks[step]["sum_sq"][:], func=ACT.Abs_reciprocal_sqrt, scale=1.0 / DH, bias=EPS
+            )
+            banks[step]["inv_rms"] = inv_rms
+
+        def apply_norm(step):
+            j = step % TOKEN_TILES
+            acc, result, inv_rms = banks[step]["acc"], banks[step]["result"], banks[step]["inv_rms"]
+            if step % SCALAR_SCALES_EVERY == SCALAR_SCALES_EVERY - 1:
+                for h in range(BLOCK_HEADS):
+                    nc.scalar.activation(
+                        out=result[:, h, j, :],
+                        in_=acc[:, DH * h : DH * (h + 1)],
+                        func=ACT.Copy,
+                        scale=inv_rms[:, h : h + 1],
+                    )
+            else:
+                nc.vector.tensor_tensor(
+                    out=result[:, :, j, :],
+                    in0=acc[:].rearrange("p (h d) -> p h d", h=BLOCK_HEADS),
+                    in1=inv_rms[:].unsqueeze(2).to_broadcast([P, BLOCK_HEADS, DH]),
+                    op=ALU.mult,
+                )
+
+        def store(step):
+            j1 = step % TOKEN_TILES + 1
+            if j1 % STORE_TILES == 0:
+                w, out, b = blocks[step // TOKEN_TILES]
+                result = banks[step]["result"]
+                for h in range(BLOCK_HEADS):
+                    by_partition = out[:, BLOCK_HEADS * b + h, :, :].rearrange("b (q j) d -> b q j d", j=TOKEN_TILES)
+                    nc.sync.dma_start(
+                        out=by_partition[:, :, j1 - STORE_TILES : j1, :].rearrange("b q j d -> b q (j d)"),
+                        in_=result[:, h, j1 - STORE_TILES : j1, :].rearrange("p j d -> p (j d)"),
+                    )
+
+        steps = len(blocks) * TOKEN_TILES
+        for step in range(steps + SCALE_LAG):
+            n, j = step // TOKEN_TILES, step % TOKEN_TILES
+            if step < steps:
+                if j == 0:
+                    w_now = w_next
+                    if n + 1 < len(blocks):
+                        w_next = new_block_tiles()
+                    result = results.tile([P, BLOCK_HEADS, TOKEN_TILES, DH], F32)
+                products(step, w_now, result)
+                sums_of_squares(step)
+            if 1 <= step <= steps:
+                inverse_rms(step - 1)
+            if step >= SCALE_LAG:
+                apply_norm(step - SCALE_LAG)
+                store(step - SCALE_LAG)
+            if n + 1 < len(blocks):
+                prepare(w_next, w_raws[n + 1], j)

@@ -24,7 +24,8 @@ BLOCKS_PER_WEIGHT = HEADS * DH // BLOCK
 EPS = 2.0 ** -23
 SCALAR_SCALES_EVERY = 3
 STORE_TILES = 4
-SCALE_LAG = 2
+SCALE_LAG = 3
+RMS_BANKS = 2
 
 FLOPS = 2 * TOKENS * C * 2 * HEADS * DH
 
@@ -73,15 +74,15 @@ def tile_pieceroutedattention_pa_kernel(tc, x, Wq, Wk, out_0, out_1):
         def new_block_tiles():
             w_codes = w_mx.tile([P, PASSES, BLOCK], U32, align_bytes=64)
             w_scales = w_mx.tile([P, PASSES, BLOCK], U8, align_bytes=64)
-            return {"codes": w_codes, "scales": w_scales, "grouped": []}
+            return {"codes": w_codes, "scales": w_scales, "grouped": {}}
 
-        def regroup(mx, pieces, g):
+        def regroup(mx, pieces, g, copy=nc.vector.tensor_copy):
             w_grouped = w_stage.tile([P, BLOCK, PACK], BF16, align_bytes=64)
-            nc.vector.tensor_copy(
+            copy(
                 out=w_grouped[:].rearrange("p (c i) t -> p c t i", i=4),
                 in_=pieces[g][:].rearrange("p t (c i) -> p c t i", i=4),
             )
-            mx["grouped"].append(w_grouped)
+            mx["grouped"][g] = w_grouped
 
         def quantise(mx, g):
             nc.vector.quantize_mx(
@@ -98,8 +99,12 @@ def tile_pieceroutedattention_pa_kernel(tc, x, Wq, Wk, out_0, out_1):
                     quantise(mx, turn // 2)
 
         w_next = new_block_tiles()
-        for turn in range(2 * PASSES):
-            prepare(w_next, w_raws[0], turn)
+        regroup(w_next, w_raws[0], 0)
+        regroup(w_next, w_raws[0], 1, copy=nc.scalar.copy)
+        quantise(w_next, 0)
+        regroup(w_next, w_raws[0], 2)
+        quantise(w_next, 2)
+        quantise(w_next, 1)
 
         x_codes = const.tile([P, PASSES, TOKENS], U32, align_bytes=64)
         x_scales = const.tile([P, PASSES, TOKENS], U8, align_bytes=64)
@@ -144,20 +149,28 @@ def tile_pieceroutedattention_pa_kernel(tc, x, Wq, Wk, out_0, out_1):
         def sums_of_squares(step):
             acc = banks[step]["acc"]
             squared = squares.tile([P, BLOCK], BF16)
-            sum_sq = norm.tile([P, BLOCK_HEADS], F32)
+            r = step % RMS_BANKS
+            if r == 0:
+                sum_sq = norm.tile([P, RMS_BANKS * BLOCK_HEADS], F32)
+            else:
+                sum_sq = banks[step - 1]["sum_sq"]
             for h in range(BLOCK_HEADS):
                 cols = slice(DH * h, DH * (h + 1))
                 nc.scalar.activation(
-                    out=squared[:, cols], in_=acc[:, cols], func=ACT.Square, accum_out=sum_sq[:, h : h + 1]
+                    out=squared[:, cols],
+                    in_=acc[:, cols],
+                    func=ACT.Square,
+                    accum_out=sum_sq[:, BLOCK_HEADS * r + h : BLOCK_HEADS * r + h + 1],
                 )
             banks[step]["sum_sq"] = sum_sq
 
-        def inverse_rms(step):
-            inv_rms = norm.tile([P, BLOCK_HEADS], F32)
+        def inverse_rms(last_step):
+            inv_rms = norm.tile([P, RMS_BANKS * BLOCK_HEADS], F32)
             nc.scalar.activation(
-                out=inv_rms[:], in_=banks[step]["sum_sq"][:], func=ACT.Abs_reciprocal_sqrt, scale=1.0 / DH, bias=EPS
+                out=inv_rms[:], in_=banks[last_step]["sum_sq"][:], func=ACT.Abs_reciprocal_sqrt, scale=1.0 / DH, bias=EPS
             )
-            banks[step]["inv_rms"] = inv_rms
+            for r in range(RMS_BANKS):
+                banks[last_step - RMS_BANKS + 1 + r]["inv_rms"] = inv_rms[:, BLOCK_HEADS * r : BLOCK_HEADS * (r + 1)]
 
         def apply_norm(step):
             j = step % TOKEN_TILES
@@ -174,7 +187,7 @@ def tile_pieceroutedattention_pa_kernel(tc, x, Wq, Wk, out_0, out_1):
                 nc.vector.tensor_tensor(
                     out=result[:, :, j, :],
                     in0=acc[:].rearrange("p (h d) -> p h d", h=BLOCK_HEADS),
-                    in1=inv_rms[:].unsqueeze(2).to_broadcast([P, BLOCK_HEADS, DH]),
+                    in1=inv_rms.unsqueeze(2).to_broadcast([P, BLOCK_HEADS, DH]),
                     op=ALU.mult,
                 )
 
@@ -201,7 +214,7 @@ def tile_pieceroutedattention_pa_kernel(tc, x, Wq, Wk, out_0, out_1):
                     result = results.tile([P, BLOCK_HEADS, TOKEN_TILES, DH], F32)
                 products(step, w_now, result)
                 sums_of_squares(step)
-            if 1 <= step <= steps:
+            if 1 <= step <= steps and step % RMS_BANKS == 0:
                 inverse_rms(step - 1)
             if step >= SCALE_LAG:
                 apply_norm(step - SCALE_LAG)

@@ -22,10 +22,16 @@ BLOCK = 512
 BLOCK_HEADS = BLOCK // DH
 BLOCKS_PER_WEIGHT = HEADS * DH // BLOCK
 EPS = 2.0 ** -23
-SCALAR_SCALES_EVERY = 3
+SCALAR_TURNS = (1, 4, 7)
+LAST_SCALAR_TURNS = (6,)
+LAST_VECTOR_SUMS = (1, 3)
 STORE_TILES = 4
 SCALE_LAG = 3
 RMS_BANKS = 2
+FIRST_PREPARATION_LAG = 2
+X_AHEAD = 4
+VECTOR_COPIES = ()
+SCALAR_COPIES = (0, 1, 2)
 
 FLOPS = 2 * TOKENS * C * 2 * HEADS * DH
 
@@ -37,7 +43,7 @@ def tile_pieceroutedattention_pa_kernel(tc, x, Wq, Wk, out_0, out_1):
     with ExitStack() as ctx:
         const = ctx.enter_context(tc.tile_pool(name="const", bufs=1))
         x_raw_pool = ctx.enter_context(tc.tile_pool(name="x_raw", bufs=TOKEN_TILES))
-        x_stage = ctx.enter_context(tc.tile_pool(name="x_stage", bufs=4))
+        x_stage = ctx.enter_context(tc.tile_pool(name="x_stage", bufs=6))
         w_raw_pool = ctx.enter_context(tc.tile_pool(name="w_raw", bufs=len(blocks) * PASSES))
         w_stage = ctx.enter_context(tc.tile_pool(name="w_stage", bufs=PASSES))
         w_mx = ctx.enter_context(tc.tile_pool(name="w_mx", bufs=2))
@@ -45,6 +51,11 @@ def tile_pieceroutedattention_pa_kernel(tc, x, Wq, Wk, out_0, out_1):
         squares = ctx.enter_context(tc.tile_pool(name="squares", bufs=4))
         results = ctx.enter_context(tc.tile_pool(name="results", bufs=3))
         psum = ctx.enter_context(tc.psum_pool(name="psum", bufs=8))
+
+        ones = const.tile([P, 1], F32)
+        nc.vector.memset(ones[:], 1.0)
+        table_warmer = const.tile([P, 1], F32)
+        nc.scalar.activation(out=table_warmer[:], in_=ones[:], func=ACT.Abs_reciprocal_sqrt)
 
         ident = const.tile([P, P], F32)
         make_identity(nc, ident[:])
@@ -92,7 +103,7 @@ def tile_pieceroutedattention_pa_kernel(tc, x, Wq, Wk, out_0, out_1):
             )
 
         def prepare(mx, pieces, turn):
-            if turn < 2 * PASSES:
+            if 0 <= turn < 2 * PASSES:
                 if turn % 2 == 0:
                     regroup(mx, pieces, turn // 2)
                 else:
@@ -108,8 +119,10 @@ def tile_pieceroutedattention_pa_kernel(tc, x, Wq, Wk, out_0, out_1):
 
         x_codes = const.tile([P, PASSES, TOKENS], U32, align_bytes=64)
         x_scales = const.tile([P, PASSES, TOKENS], U8, align_bytes=64)
-        for j0 in range(0, TOKEN_TILES, 2):
-            for g in range(PASSES):
+
+        def prepare_x(j0):
+            x_groupeds = []
+            for g in VECTOR_COPIES + SCALAR_COPIES:
                 planes = psum.tile([P, 2, 2, P], F32, tag="bank")
                 for s in range(2):
                     words = x_raws[j0 + s][:].bitcast(F32)
@@ -117,11 +130,14 @@ def tile_pieceroutedattention_pa_kernel(tc, x, Wq, Wk, out_0, out_1):
                         w0 = 2 * P * g
                         nc.tensor.transpose(planes[:, s, u, :], words[:, w0 + u : w0 + 2 * P : 2], ident[:])
                 x_grouped = x_stage.tile([P, 2 * P * PACK], BF16, align_bytes=64)
-                nc.scalar.copy(
+                copy = nc.vector.tensor_copy if g in VECTOR_COPIES else nc.scalar.copy
+                copy(
                     out=x_grouped[:].bitcast(F32).rearrange("p (s r u) -> p s r u", s=2, u=2),
                     in_=planes[:].rearrange("p s u r -> p s r u"),
                 )
-                tokens = slice(P * j0, P * (j0 + 2))
+                x_groupeds.append((g, x_grouped))
+            tokens = slice(P * j0, P * (j0 + 2))
+            for g, x_grouped in x_groupeds[1:] + x_groupeds[:1]:
                 nc.vector.quantize_mx(
                     out=x_codes[:, g, tokens].bitcast(FP8X4),
                     scales=x_scales[:, g, tokens],
@@ -148,21 +164,39 @@ def tile_pieceroutedattention_pa_kernel(tc, x, Wq, Wk, out_0, out_1):
 
         def sums_of_squares(step):
             acc = banks[step]["acc"]
-            squared = squares.tile([P, BLOCK], BF16)
             r = step % RMS_BANKS
             if r == 0:
                 sum_sq = norm.tile([P, RMS_BANKS * BLOCK_HEADS], F32)
             else:
                 sum_sq = banks[step - 1]["sum_sq"]
-            for h in range(BLOCK_HEADS):
-                cols = slice(DH * h, DH * (h + 1))
-                nc.scalar.activation(
-                    out=squared[:, cols],
-                    in_=acc[:, cols],
-                    func=ACT.Square,
-                    accum_out=sum_sq[:, BLOCK_HEADS * r + h : BLOCK_HEADS * r + h + 1],
-                )
             banks[step]["sum_sq"] = sum_sq
+            if step // TOKEN_TILES + 1 == len(blocks) and step % TOKEN_TILES in LAST_VECTOR_SUMS:
+                stats = norm.tile([P, BLOCK_HEADS, 3], F32)
+                for pair in range(BLOCK_HEADS // 2):
+                    nc.vector.bn_stats(
+                        out=stats[:, 2 * pair : 2 * pair + 2, :].rearrange("p h s -> p (h s)"),
+                        in_=acc[:, 2 * DH * pair : 2 * DH * (pair + 1)].rearrange("p (h d) -> p d h", h=2),
+                    )
+                mean_sq = norm.tile([P, BLOCK_HEADS], F32)
+                nc.vector.tensor_tensor(out=mean_sq[:], in0=stats[:, :, 1], in1=stats[:, :, 1], op=ALU.mult)
+                nc.vector.scalar_tensor_tensor(
+                    out=sum_sq[:, BLOCK_HEADS * r : BLOCK_HEADS * (r + 1)],
+                    in0=mean_sq[:],
+                    scalar=float(DH),
+                    in1=stats[:, :, 2],
+                    op0=ALU.mult,
+                    op1=ALU.add,
+                )
+            else:
+                squared = squares.tile([P, BLOCK], BF16)
+                for h in range(BLOCK_HEADS):
+                    cols = slice(DH * h, DH * (h + 1))
+                    nc.scalar.activation(
+                        out=squared[:, cols],
+                        in_=acc[:, cols],
+                        func=ACT.Square,
+                        accum_out=sum_sq[:, BLOCK_HEADS * r + h : BLOCK_HEADS * r + h + 1],
+                    )
 
         def inverse_rms(last_step):
             inv_rms = norm.tile([P, RMS_BANKS * BLOCK_HEADS], F32)
@@ -175,7 +209,7 @@ def tile_pieceroutedattention_pa_kernel(tc, x, Wq, Wk, out_0, out_1):
         def apply_norm(step):
             j = step % TOKEN_TILES
             acc, result, inv_rms = banks[step]["acc"], banks[step]["result"], banks[step]["inv_rms"]
-            if step % SCALAR_SCALES_EVERY == SCALAR_SCALES_EVERY - 1:
+            if j in (SCALAR_TURNS if step // TOKEN_TILES + 1 < len(blocks) else LAST_SCALAR_TURNS):
                 for h in range(BLOCK_HEADS):
                     nc.scalar.activation(
                         out=result[:, h, j, :],
@@ -203,9 +237,13 @@ def tile_pieceroutedattention_pa_kernel(tc, x, Wq, Wk, out_0, out_1):
                         in_=result[:, h, j1 - STORE_TILES : j1, :].rearrange("p j d -> p (j d)"),
                     )
 
+        for j0 in range(0, X_AHEAD, 2):
+            prepare_x(j0)
         steps = len(blocks) * TOKEN_TILES
         for step in range(steps + SCALE_LAG):
             n, j = step // TOKEN_TILES, step % TOKEN_TILES
+            if step % 2 == 0 and step + X_AHEAD < TOKEN_TILES:
+                prepare_x(step + X_AHEAD)
             if step < steps:
                 if j == 0:
                     w_now = w_next
@@ -220,4 +258,4 @@ def tile_pieceroutedattention_pa_kernel(tc, x, Wq, Wk, out_0, out_1):
                 apply_norm(step - SCALE_LAG)
                 store(step - SCALE_LAG)
             if n + 1 < len(blocks):
-                prepare(w_next, w_raws[n + 1], j)
+                prepare(w_next, w_raws[n + 1], j if n > 0 else j - FIRST_PREPARATION_LAG)

@@ -22,8 +22,7 @@ BLOCK = 512
 BLOCK_HEADS = BLOCK // DH
 BLOCKS_PER_WEIGHT = HEADS * DH // BLOCK
 EPS = 2.0 ** -23
-SCALAR_TURNS = (1, 4, 7)
-LAST_SCALAR_TURNS = (6,)
+SCALAR_TURNS = ((1, 4, 7), (1, 3, 5, 7), (1, 3, 5, 7), (1, 3, 5, 7), (1, 4, 7), (6,))
 LAST_VECTOR_SUMS = (1, 3)
 STORE_TILES = 4
 SCALE_LAG = 3
@@ -209,7 +208,7 @@ def tile_pieceroutedattention_pa_kernel(tc, x, Wq, Wk, out_0, out_1):
         def apply_norm(step):
             j = step % TOKEN_TILES
             acc, result, inv_rms = banks[step]["acc"], banks[step]["result"], banks[step]["inv_rms"]
-            if j in (SCALAR_TURNS if step // TOKEN_TILES + 1 < len(blocks) else LAST_SCALAR_TURNS):
+            if j in SCALAR_TURNS[step // TOKEN_TILES]:
                 for h in range(BLOCK_HEADS):
                     nc.scalar.activation(
                         out=result[:, h, j, :],

@@ -21,16 +21,17 @@ PASSES = C // K_PASS
 BLOCK = 512
 BLOCK_HEADS = BLOCK // DH
 BLOCKS_PER_WEIGHT = HEADS * DH // BLOCK
+BLOCKS = 2 * BLOCKS_PER_WEIGHT
+STEPS = BLOCKS * TOKEN_TILES
 EPS = 2.0 ** -23
-SCALAR_TURNS = ((1, 4, 7), (1, 3, 5, 7), (1, 3, 5, 7), (1, 3, 5, 7), (1, 4, 7), (6,))
-LAST_VECTOR_SUMS = (1, 3)
+
+SCALAR_NORM_TILES = ((1, 4, 7), (1, 3, 5, 7), (1, 4, 7), (1, 3, 5, 7), (1, 4, 7), (6,))
+VECTOR_SUMS_TILES = (1, 3)
 STORE_TILES = 4
-SCALE_LAG = 3
+NORM_LAG = 3
 RMS_BANKS = 2
-FIRST_PREPARATION_LAG = 2
 X_AHEAD = 4
-VECTOR_COPIES = ()
-SCALAR_COPIES = (0, 1, 2)
+FIRST_PREPARATION_LAG = 2
 
 FLOPS = 2 * TOKENS * C * 2 * HEADS * DH
 
@@ -42,8 +43,8 @@ def tile_pieceroutedattention_pa_kernel(tc, x, Wq, Wk, out_0, out_1):
     with ExitStack() as ctx:
         const = ctx.enter_context(tc.tile_pool(name="const", bufs=1))
         x_raw_pool = ctx.enter_context(tc.tile_pool(name="x_raw", bufs=TOKEN_TILES))
-        x_stage = ctx.enter_context(tc.tile_pool(name="x_stage", bufs=6))
-        w_raw_pool = ctx.enter_context(tc.tile_pool(name="w_raw", bufs=len(blocks) * PASSES))
+        w_raw_pool = ctx.enter_context(tc.tile_pool(name="w_raw", bufs=BLOCKS * PASSES))
+        x_stage = ctx.enter_context(tc.tile_pool(name="x_stage", bufs=2 * PASSES))
         w_stage = ctx.enter_context(tc.tile_pool(name="w_stage", bufs=PASSES))
         w_mx = ctx.enter_context(tc.tile_pool(name="w_mx", bufs=2))
         norm = ctx.enter_context(tc.tile_pool(name="norm", bufs=8))
@@ -60,7 +61,7 @@ def tile_pieceroutedattention_pa_kernel(tc, x, Wq, Wk, out_0, out_1):
         make_identity(nc, ident[:])
 
         def load_block(w, b):
-            pieces = []
+            w_raws = []
             for g in range(PASSES):
                 w_raw = w_raw_pool.tile([P, PACK, BLOCK], BF16)
                 k0 = K_PASS * g
@@ -68,10 +69,10 @@ def tile_pieceroutedattention_pa_kernel(tc, x, Wq, Wk, out_0, out_1):
                     out=w_raw[:],
                     in_=w[k0 : k0 + K_PASS, BLOCK * b : BLOCK * (b + 1)].rearrange("(q t) c -> q t c", t=PACK),
                 )
-                pieces.append(w_raw)
-            return pieces
+                w_raws.append(w_raw)
+            return w_raws
 
-        w_raws = [load_block(blocks[0][0], blocks[0][2])]
+        block_raws = [load_block(Wq, 0)]
         x_by_tile = x.rearrange("b (q j) c -> (b q) j c", j=TOKEN_TILES)
         x_raws = []
         for j in range(TOKEN_TILES):
@@ -79,18 +80,18 @@ def tile_pieceroutedattention_pa_kernel(tc, x, Wq, Wk, out_0, out_1):
             nc.sync.dma_start(out=x_raw[:], in_=x_by_tile[:, j, :])
             x_raws.append(x_raw)
         for w, out, b in blocks[1:]:
-            w_raws.append(load_block(w, b))
+            block_raws.append(load_block(w, b))
 
         def new_block_tiles():
             w_codes = w_mx.tile([P, PASSES, BLOCK], U32, align_bytes=64)
             w_scales = w_mx.tile([P, PASSES, BLOCK], U8, align_bytes=64)
             return {"codes": w_codes, "scales": w_scales, "grouped": {}}
 
-        def regroup(mx, pieces, g, copy=nc.vector.tensor_copy):
+        def regroup(mx, w_raws, g, copy):
             w_grouped = w_stage.tile([P, BLOCK, PACK], BF16, align_bytes=64)
             copy(
                 out=w_grouped[:].rearrange("p (c i) t -> p c t i", i=4),
-                in_=pieces[g][:].rearrange("p t (c i) -> p c t i", i=4),
+                in_=w_raws[g][:].rearrange("p t (c i) -> p c t i", i=4),
             )
             mx["grouped"][g] = w_grouped
 
@@ -101,27 +102,28 @@ def tile_pieceroutedattention_pa_kernel(tc, x, Wq, Wk, out_0, out_1):
                 in_=mx["grouped"][g][:].rearrange("p c t -> p (c t)"),
             )
 
-        def prepare(mx, pieces, turn):
+        def prepare(mx, w_raws, turn):
             if 0 <= turn < 2 * PASSES:
                 if turn % 2 == 0:
-                    regroup(mx, pieces, turn // 2)
+                    regroup(mx, w_raws, turn // 2, nc.vector.tensor_copy)
                 else:
                     quantise(mx, turn // 2)
 
-        w_next = new_block_tiles()
-        regroup(w_next, w_raws[0], 0)
-        regroup(w_next, w_raws[0], 1, copy=nc.scalar.copy)
-        quantise(w_next, 0)
-        regroup(w_next, w_raws[0], 2)
-        quantise(w_next, 2)
-        quantise(w_next, 1)
+        mx_next = new_block_tiles()
+        regroup(mx_next, block_raws[0], 0, nc.vector.tensor_copy)
+        regroup(mx_next, block_raws[0], 1, nc.scalar.copy)
+        quantise(mx_next, 0)
+        regroup(mx_next, block_raws[0], 2, nc.vector.tensor_copy)
+        quantise(mx_next, 2)
+        quantise(mx_next, 1)
 
         x_codes = const.tile([P, PASSES, TOKENS], U32, align_bytes=64)
         x_scales = const.tile([P, PASSES, TOKENS], U8, align_bytes=64)
 
         def prepare_x(j0):
+            tokens = slice(P * j0, P * (j0 + 2))
             x_groupeds = []
-            for g in VECTOR_COPIES + SCALAR_COPIES:
+            for g in range(PASSES):
                 planes = psum.tile([P, 2, 2, P], F32, tag="bank")
                 for s in range(2):
                     words = x_raws[j0 + s][:].bitcast(F32)
@@ -129,18 +131,16 @@ def tile_pieceroutedattention_pa_kernel(tc, x, Wq, Wk, out_0, out_1):
                         w0 = 2 * P * g
                         nc.tensor.transpose(planes[:, s, u, :], words[:, w0 + u : w0 + 2 * P : 2], ident[:])
                 x_grouped = x_stage.tile([P, 2 * P * PACK], BF16, align_bytes=64)
-                copy = nc.vector.tensor_copy if g in VECTOR_COPIES else nc.scalar.copy
-                copy(
+                nc.scalar.copy(
                     out=x_grouped[:].bitcast(F32).rearrange("p (s r u) -> p s r u", s=2, u=2),
                     in_=planes[:].rearrange("p s u r -> p s r u"),
                 )
-                x_groupeds.append((g, x_grouped))
-            tokens = slice(P * j0, P * (j0 + 2))
-            for g, x_grouped in x_groupeds[1:] + x_groupeds[:1]:
+                x_groupeds.append(x_grouped)
+            for g in range(PASSES):
                 nc.vector.quantize_mx(
                     out=x_codes[:, g, tokens].bitcast(FP8X4),
                     scales=x_scales[:, g, tokens],
-                    in_=x_grouped[:],
+                    in_=x_groupeds[g][:],
                 )
 
         banks = {}
@@ -169,7 +169,7 @@ def tile_pieceroutedattention_pa_kernel(tc, x, Wq, Wk, out_0, out_1):
             else:
                 sum_sq = banks[step - 1]["sum_sq"]
             banks[step]["sum_sq"] = sum_sq
-            if step // TOKEN_TILES + 1 == len(blocks) and step % TOKEN_TILES in LAST_VECTOR_SUMS:
+            if step // TOKEN_TILES == BLOCKS - 1 and step % TOKEN_TILES in VECTOR_SUMS_TILES:
                 stats = norm.tile([P, BLOCK_HEADS, 3], F32)
                 for pair in range(BLOCK_HEADS // 2):
                     nc.vector.bn_stats(
@@ -206,9 +206,9 @@ def tile_pieceroutedattention_pa_kernel(tc, x, Wq, Wk, out_0, out_1):
                 banks[last_step - RMS_BANKS + 1 + r]["inv_rms"] = inv_rms[:, BLOCK_HEADS * r : BLOCK_HEADS * (r + 1)]
 
         def apply_norm(step):
-            j = step % TOKEN_TILES
+            n, j = step // TOKEN_TILES, step % TOKEN_TILES
             acc, result, inv_rms = banks[step]["acc"], banks[step]["result"], banks[step]["inv_rms"]
-            if j in SCALAR_TURNS[step // TOKEN_TILES]:
+            if j in SCALAR_NORM_TILES[n]:
                 for h in range(BLOCK_HEADS):
                     nc.scalar.activation(
                         out=result[:, h, j, :],
@@ -238,23 +238,22 @@ def tile_pieceroutedattention_pa_kernel(tc, x, Wq, Wk, out_0, out_1):
 
         for j0 in range(0, X_AHEAD, 2):
             prepare_x(j0)
-        steps = len(blocks) * TOKEN_TILES
-        for step in range(steps + SCALE_LAG):
+        for step in range(STEPS + NORM_LAG):
             n, j = step // TOKEN_TILES, step % TOKEN_TILES
             if step % 2 == 0 and step + X_AHEAD < TOKEN_TILES:
                 prepare_x(step + X_AHEAD)
-            if step < steps:
+            if step < STEPS:
                 if j == 0:
-                    w_now = w_next
-                    if n + 1 < len(blocks):
-                        w_next = new_block_tiles()
+                    mx_now = mx_next
+                    if n + 1 < BLOCKS:
+                        mx_next = new_block_tiles()
                     result = results.tile([P, BLOCK_HEADS, TOKEN_TILES, DH], F32)
-                products(step, w_now, result)
+                products(step, mx_now, result)
                 sums_of_squares(step)
-            if 1 <= step <= steps and step % RMS_BANKS == 0:
+            if 1 <= step <= STEPS and step % RMS_BANKS == 0:
                 inverse_rms(step - 1)
-            if step >= SCALE_LAG:
-                apply_norm(step - SCALE_LAG)
-                store(step - SCALE_LAG)
-            if n + 1 < len(blocks):
-                prepare(w_next, w_raws[n + 1], j if n > 0 else j - FIRST_PREPARATION_LAG)
+            if step >= NORM_LAG:
+                apply_norm(step - NORM_LAG)
+                store(step - NORM_LAG)
+            if n + 1 < BLOCKS:
+                prepare(mx_next, block_raws[n + 1], j if n > 0 else j - FIRST_PREPARATION_LAG)

@@ -30,8 +30,8 @@ VECTOR_SUMS_TILES = (1, 3)
 STORE_TILES = 4
 NORM_LAG = 3
 RMS_BANKS = 2
-X_AHEAD = 4
-FIRST_PREPARATION_LAG = 2
+X_PAIR_AFTER_STEP = {1: 4, 3: 6}
+FIRST_TURNS = {0: 0, 1: 1, 2: 2, 3: 3, 5: 4, 6: 5}
 
 FLOPS = 2 * TOKENS * C * 2 * HEADS * DH
 
@@ -60,27 +60,37 @@ def tile_pieceroutedattention_pa_kernel(tc, x, Wq, Wk, out_0, out_1):
         ident = const.tile([P, P], F32)
         make_identity(nc, ident[:])
 
-        def load_block(w, b):
-            w_raws = []
-            for g in range(PASSES):
-                w_raw = w_raw_pool.tile([P, PACK, BLOCK], BF16)
-                k0 = K_PASS * g
-                nc.sync.dma_start(
-                    out=w_raw[:],
-                    in_=w[k0 : k0 + K_PASS, BLOCK * b : BLOCK * (b + 1)].rearrange("(q t) c -> q t c", t=PACK),
-                )
-                w_raws.append(w_raw)
-            return w_raws
-
-        block_raws = [load_block(Wq, 0)]
-        x_by_tile = x.rearrange("b (q j) c -> (b q) j c", j=TOKEN_TILES)
+        block_raws = [[] for n in range(BLOCKS)]
         x_raws = []
-        for j in range(TOKEN_TILES):
+        x_by_tile = x.rearrange("b (q j) c -> (b q) j c", j=TOKEN_TILES)
+
+        def load_pass(n):
+            w, out, b = blocks[n]
+            w_raw = w_raw_pool.tile([P, PACK, BLOCK], BF16)
+            k0 = K_PASS * len(block_raws[n])
+            nc.sync.dma_start(
+                out=w_raw[:],
+                in_=w[k0 : k0 + K_PASS, BLOCK * b : BLOCK * (b + 1)].rearrange("(q t) c -> q t c", t=PACK),
+            )
+            block_raws[n].append(w_raw)
+
+        def load_x():
             x_raw = x_raw_pool.tile([P, C], BF16)
-            nc.sync.dma_start(out=x_raw[:], in_=x_by_tile[:, j, :])
+            nc.sync.dma_start(out=x_raw[:], in_=x_by_tile[:, len(x_raws), :])
             x_raws.append(x_raw)
-        for w, out, b in blocks[1:]:
-            block_raws.append(load_block(w, b))
+
+        for g in range(PASSES):
+            load_pass(0)
+        for j in range(TOKEN_TILES - 2):
+            load_x()
+        load_pass(1)
+        load_x()
+        load_x()
+        load_pass(1)
+        load_pass(1)
+        for n in range(2, BLOCKS):
+            for g in range(PASSES):
+                load_pass(n)
 
         def new_block_tiles():
             w_codes = w_mx.tile([P, PASSES, BLOCK], U32, align_bytes=64)
@@ -236,12 +246,10 @@ def tile_pieceroutedattention_pa_kernel(tc, x, Wq, Wk, out_0, out_1):
                         in_=result[:, h, j1 - STORE_TILES : j1, :].rearrange("p j d -> p (j d)"),
                     )
 
-        for j0 in range(0, X_AHEAD, 2):
-            prepare_x(j0)
+        prepare_x(0)
+        prepare_x(2)
         for step in range(STEPS + NORM_LAG):
             n, j = step // TOKEN_TILES, step % TOKEN_TILES
-            if step % 2 == 0 and step + X_AHEAD < TOKEN_TILES:
-                prepare_x(step + X_AHEAD)
             if step < STEPS:
                 if j == 0:
                     mx_now = mx_next
@@ -249,6 +257,8 @@ def tile_pieceroutedattention_pa_kernel(tc, x, Wq, Wk, out_0, out_1):
                         mx_next = new_block_tiles()
                     result = results.tile([P, BLOCK_HEADS, TOKEN_TILES, DH], F32)
                 products(step, mx_now, result)
+                if step in X_PAIR_AFTER_STEP:
+                    prepare_x(X_PAIR_AFTER_STEP[step])
                 sums_of_squares(step)
             if 1 <= step <= STEPS and step % RMS_BANKS == 0:
                 inverse_rms(step - 1)
@@ -256,4 +266,4 @@ def tile_pieceroutedattention_pa_kernel(tc, x, Wq, Wk, out_0, out_1):
                 apply_norm(step - NORM_LAG)
                 store(step - NORM_LAG)
             if n + 1 < BLOCKS:
-                prepare(mx_next, block_raws[n + 1], j if n > 0 else j - FIRST_PREPARATION_LAG)
+                prepare(mx_next, block_raws[n + 1], j if n > 0 else FIRST_TURNS.get(j, -1))

from contextlib import ExitStack

import concourse.mybir as mybir
from concourse.masks import make_identity

F32 = mybir.dt.float32
BF16 = mybir.dt.bfloat16
U32 = mybir.dt.uint32
U8 = mybir.dt.uint8
FP8X4 = mybir.dt.float8_e4m3fn_x4
ACT = mybir.ActivationFunctionType
ALU = mybir.AluOpType

P = 128
PACK = 4
K_PASS = P * PACK
BOARDS, SQUARES, C, HEADS, DH = 16, 64, 1536, 12, 128
TOKENS = BOARDS * SQUARES
TOKEN_TILES = TOKENS // P
PASSES = C // K_PASS
BLOCK = 512
BLOCK_HEADS = BLOCK // DH
BLOCKS_PER_WEIGHT = HEADS * DH // BLOCK
BLOCKS = 2 * BLOCKS_PER_WEIGHT
STEPS = BLOCKS * TOKEN_TILES
EPS = 2.0 ** -23

SCALAR_NORM_TILES = ((1, 4, 7), (1, 3, 5, 7), (1, 4, 7), (1, 3, 5, 7), (1, 4, 7), (6,))
VECTOR_SUMS_TILES = (1, 3)
STORE_TILES = 4
NORM_LAG = 3
RMS_BANKS = 2
X_PAIR_AFTER_STEP = {1: 4, 3: 6}
FIRST_TURNS = {0: 0, 1: 1, 2: 2, 3: 3, 5: 4, 6: 5}

FLOPS = 2 * TOKENS * C * 2 * HEADS * DH


def tile_pieceroutedattention_pa_kernel(tc, x, Wq, Wk, out_0, out_1):
    nc = tc.nc
    blocks = [(w, out, b) for (w, out) in ((Wq, out_0), (Wk, out_1)) for b in range(BLOCKS_PER_WEIGHT)]

    with ExitStack() as ctx:
        const = ctx.enter_context(tc.tile_pool(name="const", bufs=1))
        x_raw_pool = ctx.enter_context(tc.tile_pool(name="x_raw", bufs=TOKEN_TILES))
        w_raw_pool = ctx.enter_context(tc.tile_pool(name="w_raw", bufs=BLOCKS * PASSES))
        x_stage = ctx.enter_context(tc.tile_pool(name="x_stage", bufs=2 * PASSES))
        w_stage = ctx.enter_context(tc.tile_pool(name="w_stage", bufs=PASSES))
        w_mx = ctx.enter_context(tc.tile_pool(name="w_mx", bufs=2))
        norm = ctx.enter_context(tc.tile_pool(name="norm", bufs=8))
        squares = ctx.enter_context(tc.tile_pool(name="squares", bufs=4))
        results = ctx.enter_context(tc.tile_pool(name="results", bufs=3))
        psum = ctx.enter_context(tc.psum_pool(name="psum", bufs=8))

        ones = const.tile([P, 1], F32)
        nc.vector.memset(ones[:], 1.0)
        table_warmer = const.tile([P, 1], F32)
        nc.scalar.activation(out=table_warmer[:], in_=ones[:], func=ACT.Abs_reciprocal_sqrt)

        ident = const.tile([P, P], F32)
        make_identity(nc, ident[:])

        block_raws = [[] for n in range(BLOCKS)]
        x_raws = []
        x_by_tile = x.rearrange("b (q j) c -> (b q) j c", j=TOKEN_TILES)

        def load_pass(n):
            w, out, b = blocks[n]
            w_raw = w_raw_pool.tile([P, PACK, BLOCK], BF16)
            k0 = K_PASS * len(block_raws[n])
            nc.sync.dma_start(
                out=w_raw[:],
                in_=w[k0 : k0 + K_PASS, BLOCK * b : BLOCK * (b + 1)].rearrange("(q t) c -> q t c", t=PACK),
            )
            block_raws[n].append(w_raw)

        def load_x():
            x_raw = x_raw_pool.tile([P, C], BF16)
            nc.sync.dma_start(out=x_raw[:], in_=x_by_tile[:, len(x_raws), :])
            x_raws.append(x_raw)

        for g in range(PASSES):
            load_pass(0)
        for j in range(TOKEN_TILES - 2):
            load_x()
        load_pass(1)
        load_x()
        load_x()
        load_pass(1)
        load_pass(1)
        for n in range(2, BLOCKS):
            for g in range(PASSES):
                load_pass(n)

        def new_block_tiles():
            w_codes = w_mx.tile([P, PASSES, BLOCK], U32, align_bytes=64)
            w_scales = w_mx.tile([P, PASSES, BLOCK], U8, align_bytes=64)
            return {"codes": w_codes, "scales": w_scales, "grouped": {}}

        def regroup(mx, w_raws, g, copy):
            w_grouped = w_stage.tile([P, BLOCK, PACK], BF16, align_bytes=64)
            copy(
                out=w_grouped[:].rearrange("p (c i) t -> p c t i", i=4),
                in_=w_raws[g][:].rearrange("p t (c i) -> p c t i", i=4),
            )
            mx["grouped"][g] = w_grouped

        def quantise(mx, g):
            nc.vector.quantize_mx(
                out=mx["codes"][:, g, :].bitcast(FP8X4),
                scales=mx["scales"][:, g, :],
                in_=mx["grouped"][g][:].rearrange("p c t -> p (c t)"),
            )

        def prepare(mx, w_raws, turn):
            if 0 <= turn < 2 * PASSES:
                if turn % 2 == 0:
                    regroup(mx, w_raws, turn // 2, nc.vector.tensor_copy)
                else:
                    quantise(mx, turn // 2)

        mx_next = new_block_tiles()
        regroup(mx_next, block_raws[0], 0, nc.vector.tensor_copy)
        regroup(mx_next, block_raws[0], 1, nc.scalar.copy)
        quantise(mx_next, 0)
        regroup(mx_next, block_raws[0], 2, nc.vector.tensor_copy)
        quantise(mx_next, 2)
        quantise(mx_next, 1)

        x_codes = const.tile([P, PASSES, TOKENS], U32, align_bytes=64)
        x_scales = const.tile([P, PASSES, TOKENS], U8, align_bytes=64)

        def prepare_x(j0):
            tokens = slice(P * j0, P * (j0 + 2))
            x_groupeds = []
            for g in range(PASSES):
                planes = psum.tile([P, 2, 2, P], F32, tag="bank")
                for s in range(2):
                    words = x_raws[j0 + s][:].bitcast(F32)
                    for u in range(2):
                        w0 = 2 * P * g
                        nc.tensor.transpose(planes[:, s, u, :], words[:, w0 + u : w0 + 2 * P : 2], ident[:])
                x_grouped = x_stage.tile([P, 2 * P * PACK], BF16, align_bytes=64)
                nc.scalar.copy(
                    out=x_grouped[:].bitcast(F32).rearrange("p (s r u) -> p s r u", s=2, u=2),
                    in_=planes[:].rearrange("p s u r -> p s r u"),
                )
                x_groupeds.append(x_grouped)
            for g in range(PASSES):
                nc.vector.quantize_mx(
                    out=x_codes[:, g, tokens].bitcast(FP8X4),
                    scales=x_scales[:, g, tokens],
                    in_=x_groupeds[g][:],
                )

        banks = {}

        def products(step, mx, result):
            j = step % TOKEN_TILES
            tokens = slice(P * j, P * (j + 1))
            acc = psum.tile([P, BLOCK], F32, tag="bank")
            for g in range(PASSES):
                nc.tensor.matmul_mx(
                    out=acc[:],
                    lhsT=x_codes[:, g, tokens].bitcast(FP8X4),
                    lhsT_scale=x_scales[:, g, tokens],
                    rhs=mx["codes"][:, g, :].bitcast(FP8X4),
                    rhs_scale=mx["scales"][:, g, :],
                    start=(g == 0),
                    stop=(g == PASSES - 1),
                )
            banks[step] = {"acc": acc, "result": result}

        def sums_of_squares(step):
            acc = banks[step]["acc"]
            r = step % RMS_BANKS
            if r == 0:
                sum_sq = norm.tile([P, RMS_BANKS * BLOCK_HEADS], F32)
            else:
                sum_sq = banks[step - 1]["sum_sq"]
            banks[step]["sum_sq"] = sum_sq
            if step // TOKEN_TILES == BLOCKS - 1 and step % TOKEN_TILES in VECTOR_SUMS_TILES:
                stats = norm.tile([P, BLOCK_HEADS, 3], F32)
                for pair in range(BLOCK_HEADS // 2):
                    nc.vector.bn_stats(
                        out=stats[:, 2 * pair : 2 * pair + 2, :].rearrange("p h s -> p (h s)"),
                        in_=acc[:, 2 * DH * pair : 2 * DH * (pair + 1)].rearrange("p (h d) -> p d h", h=2),
                    )
                mean_sq = norm.tile([P, BLOCK_HEADS], F32)
                nc.vector.tensor_tensor(out=mean_sq[:], in0=stats[:, :, 1], in1=stats[:, :, 1], op=ALU.mult)
                nc.vector.scalar_tensor_tensor(
                    out=sum_sq[:, BLOCK_HEADS * r : BLOCK_HEADS * (r + 1)],
                    in0=mean_sq[:],
                    scalar=float(DH),
                    in1=stats[:, :, 2],
                    op0=ALU.mult,
                    op1=ALU.add,
                )
            else:
                squared = squares.tile([P, BLOCK], BF16)
                for h in range(BLOCK_HEADS):
                    cols = slice(DH * h, DH * (h + 1))
                    nc.scalar.activation(
                        out=squared[:, cols],
                        in_=acc[:, cols],
                        func=ACT.Square,
                        accum_out=sum_sq[:, BLOCK_HEADS * r + h : BLOCK_HEADS * r + h + 1],
                    )

        def inverse_rms(last_step):
            inv_rms = norm.tile([P, RMS_BANKS * BLOCK_HEADS], F32)
            nc.scalar.activation(
                out=inv_rms[:], in_=banks[last_step]["sum_sq"][:], func=ACT.Abs_reciprocal_sqrt, scale=1.0 / DH, bias=EPS
            )
            for r in range(RMS_BANKS):
                banks[last_step - RMS_BANKS + 1 + r]["inv_rms"] = inv_rms[:, BLOCK_HEADS * r : BLOCK_HEADS * (r + 1)]

        def apply_norm(step):
            n, j = step // TOKEN_TILES, step % TOKEN_TILES
            acc, result, inv_rms = banks[step]["acc"], banks[step]["result"], banks[step]["inv_rms"]
            if j in SCALAR_NORM_TILES[n]:
                for h in range(BLOCK_HEADS):
                    nc.scalar.activation(
                        out=result[:, h, j, :],
                        in_=acc[:, DH * h : DH * (h + 1)],
                        func=ACT.Copy,
                        scale=inv_rms[:, h : h + 1],
                    )
            else:
                nc.vector.tensor_tensor(
                    out=result[:, :, j, :],
                    in0=acc[:].rearrange("p (h d) -> p h d", h=BLOCK_HEADS),
                    in1=inv_rms.unsqueeze(2).to_broadcast([P, BLOCK_HEADS, DH]),
                    op=ALU.mult,
                )

        def store(step):
            j1 = step % TOKEN_TILES + 1
            if j1 % STORE_TILES == 0:
                w, out, b = blocks[step // TOKEN_TILES]
                result = banks[step]["result"]
                for h in range(BLOCK_HEADS):
                    by_partition = out[:, BLOCK_HEADS * b + h, :, :].rearrange("b (q j) d -> b q j d", j=TOKEN_TILES)
                    nc.sync.dma_start(
                        out=by_partition[:, :, j1 - STORE_TILES : j1, :].rearrange("b q j d -> b q (j d)"),
                        in_=result[:, h, j1 - STORE_TILES : j1, :].rearrange("p j d -> p (j d)"),
                    )

        prepare_x(0)
        prepare_x(2)
        for step in range(STEPS + NORM_LAG):
            n, j = step // TOKEN_TILES, step % TOKEN_TILES
            if step < STEPS:
                if j == 0:
                    mx_now = mx_next
                    if n + 1 < BLOCKS:
                        mx_next = new_block_tiles()
                    result = results.tile([P, BLOCK_HEADS, TOKEN_TILES, DH], F32)
                products(step, mx_now, result)
                if step in X_PAIR_AFTER_STEP:
                    prepare_x(X_PAIR_AFTER_STEP[step])
                sums_of_squares(step)
            if 1 <= step <= STEPS and step % RMS_BANKS == 0:
                inverse_rms(step - 1)
            if step >= NORM_LAG:
                apply_norm(step - NORM_LAG)
                store(step - NORM_LAG)
            if n + 1 < BLOCKS:
                prepare(mx_next, block_raws[n + 1], j if n > 0 else FIRST_TURNS.get(j, -1))
